import numpy as np
import ml_dtypes


def mxq(x, axis, fmt="e4m3"):
    dtype, down = {"e4m3": (ml_dtypes.float8_e4m3fn, 7), "e5m2": (ml_dtypes.float8_e5m2, 14)}[fmt]
    v = np.moveaxis(np.asarray(x, np.float32).astype(ml_dtypes.bfloat16).astype(np.float64), axis, -1)
    blocks = v.reshape(v.shape[:-1] + (-1, 32))
    amax = np.abs(blocks).max(-1, keepdims=True)
    byte = np.maximum(np.where(amax > 0, np.frexp(amax)[1] - 1 + 127, 0) - down, 1)
    scale = np.exp2(byte - 127.0)
    codes = (blocks / scale).astype(np.float32).astype(dtype).astype(np.float64)
    return np.moveaxis((codes * scale).reshape(v.shape), -1, axis)


WIDE = False


def mx_kscale(k):
    if not WIDE:
        return np.ones(k)
    levels = np.array([10, -10, 5, -5, 0])
    a = np.random.permutation(np.resize(levels, k // 512 * 4)).reshape(k // 512, 4)
    idx = np.arange(k)
    return np.exp2(a[idx // 512, idx % 128 // 32])


BF16 = ml_dtypes.bfloat16


def bf(x):
    return np.asarray(x, np.float32).astype(BF16)


def f64(x):
    return np.asarray(x).astype(np.float64)


B, S, D, H, DH, DV, R = 4, 2048, 512, 2, 64, 64, 512
EPS = 1e-6
ROPE_THETA = 10000.0


def rms_norm(c, w):
    var = np.mean(np.square(c), axis=-1, keepdims=True)
    return c * (1.0 / np.sqrt(var + EPS)) * w


def apply_rope(t, cos, sin):
    b, s, h, d = t.shape
    tr = t.reshape(b, s, h, d // 2, 2)
    x1, x2 = tr[..., 0], tr[..., 1]
    c = cos[None, :, None, :]
    sn = sin[None, :, None, :]
    o1 = x1 * c - x2 * sn
    o2 = x1 * sn + x2 * c
    return np.stack([o1, o2], axis=-1).reshape(b, s, h, d)


def setup_inputs():
    s = mx_kscale(D)
    t = mx_kscale(R)
    inv_freq = 1.0 / ROPE_THETA ** (np.arange(0, DH, 2) / DH)
    ang = np.arange(S)[:, None] * inv_freq[None, :]
    return {"x": bf(np.random.standard_normal((B, S, D)) * s),
            "freqs_cos": bf(np.cos(ang)),
            "freqs_sin": bf(np.sin(ang)),
            "w_kv_compress": bf(np.random.standard_normal((D, R)) / np.sqrt(D) / s[:, None]),
            "kv_norm_w": bf((1.0 + 0.1 * np.random.standard_normal(R)) * t),
            "w_k_up": bf(np.random.standard_normal((R, H * DH)) / np.sqrt(R) / t[:, None]),
            "w_v_up": bf(np.random.standard_normal((R, H * DV)) / np.sqrt(R) / t[:, None])}


def reference(x, freqs_cos, freqs_sin, w_kv_compress, kv_norm_w, w_k_up, w_v_up):
    c = mxq(f64(x), 2, "e4m3") @ mxq(f64(w_kv_compress), 0, "e4m3")
    latent_q = mxq(rms_norm(c, f64(kv_norm_w)), 2, "e4m3")
    k = (latent_q @ mxq(f64(w_k_up), 0, "e4m3")).reshape(B, S, H, DH)
    v = (latent_q @ mxq(f64(w_v_up), 0, "e4m3")).reshape(B, S, H, DV)
    return apply_rope(k, f64(freqs_cos), f64(freqs_sin)), v

@@ -1,0 +1,339 @@
+from contextlib import ExitStack
+
+import concourse.mybir as mybir
+from concourse.masks import make_identity
+
+F32 = mybir.dt.float32
+BF16 = mybir.dt.bfloat16
+U32 = mybir.dt.uint32
+U8 = mybir.dt.uint8
+FP8X4 = mybir.dt.float8_e4m3fn_x4
+FUNC = mybir.ActivationFunctionType
+ALU = mybir.AluOpType
+
+P = 128
+PACK = 4
+BATCH, SEQ, D_MODEL, D_LATENT = 4, 2048, 512, 512
+HEADS, D_HEAD = 2, 64
+D_K = HEADS * D_HEAD
+D_KV = 2 * D_K
+FREQS = D_HEAD // 2
+PAIRS = HEADS * FREQS
+EPS = 1e-6
+
+TILES_PER_BATCH = SEQ // P
+ROUND_TILES = 2
+ROUNDS_PER_BATCH = TILES_PER_BATCH // ROUND_TILES
+ROUNDS = BATCH * ROUNDS_PER_BATCH
+CHUNK_ROUNDS = 2
+CHUNKS = ROUNDS // CHUNK_ROUNDS
+CHUNKS_PER_BATCH = CHUNKS // BATCH
+ROUND_X = ROUND_TILES * D_MODEL
+BANK_F32 = 512
+
+FLOPS = 2 * BATCH * SEQ * D_MODEL * D_LATENT + 2 * BATCH * SEQ * D_LATENT * D_KV
+
+
+def tile_mla_pa_t_kernel(
+    tc, x, freqs_cos, freqs_sin, w_kv_compress, kv_norm_w, w_k_up, w_v_up, out_0, out_1
+):
+    nc = tc.nc
+    with ExitStack() as stack:
+        stack.enter_context(tc.manual_schedule())
+        consts = stack.enter_context(tc.tile_pool(name="consts", bufs=1))
+        x_pool = stack.enter_context(tc.tile_pool(name="x_pool", bufs=CHUNKS))
+        work = stack.enter_context(tc.tile_pool(name="work", bufs=3))
+        psum = stack.enter_context(tc.psum_pool(name="psum", bufs=1))
+
+        x_rows = x.rearrange("b (p g) d -> b p (g d)", g=TILES_PER_BATCH)
+        k_rows = out_0.rearrange("b (p g) h d -> b p (g h d)", g=TILES_PER_BATCH)
+        v_rows = out_1.rearrange("b (p g) h d -> b p (g h d)", g=TILES_PER_BATCH)
+
+        def load_weight(queue, raw, weight):
+            queue.dma_start(
+                out=raw[:].rearrange("q (u ec) -> q u ec", u=2),
+                in_=weight.rearrange("(u q e) c -> q u (e c)", u=2, e=2),
+            )
+
+        wc_raw = consts.tile([P, PACK * D_LATENT], BF16)
+        wk_raw = consts.tile([P, PACK * D_K], BF16)
+        wv_raw = consts.tile([P, PACK * D_K], BF16)
+        gain = consts.tile([P, D_LATENT], BF16)
+        cos_sb = consts.tile([P, TILES_PER_BATCH * FREQS], BF16)
+        sin_sb = consts.tile([P, TILES_PER_BATCH * FREQS], BF16)
+
+        def load_x_chunk(chunk):
+            x_chunk = x_pool.tile([P, CHUNK_ROUNDS * ROUND_X], BF16)
+            first = (chunk % CHUNKS_PER_BATCH) * CHUNK_ROUNDS * ROUND_X
+            nc.sync.dma_start(
+                out=x_chunk[:],
+                in_=x_rows[chunk // CHUNKS_PER_BATCH, :, first : first + CHUNK_ROUNDS * ROUND_X],
+            )
+            return x_chunk
+
+        load_weight(nc.sync, wc_raw, w_kv_compress)
+        x_chunks = [load_x_chunk(0)]
+        load_weight(nc.sync, wk_raw, w_k_up)
+        load_weight(nc.sync, wv_raw, w_v_up)
+        nc.sync.dma_start(out=gain[:], in_=kv_norm_w.partition_broadcast(P))
+        x_chunks.append(load_x_chunk(1))
+        nc.sync.dma_start(
+            out=cos_sb[:], in_=freqs_cos.rearrange("(p g) i -> p (g i)", g=TILES_PER_BATCH)
+        )
+        nc.sync.dma_start(
+            out=sin_sb[:], in_=freqs_sin.rearrange("(p g) i -> p (g i)", g=TILES_PER_BATCH)
+        )
+        for chunk in range(2, CHUNKS):
+            x_chunks.append(load_x_chunk(chunk))
+
+        ident = consts.tile([P, P], F32)
+        make_identity(nc, ident[:])
+        one = consts.tile([P, 1], F32)
+        nc.vector.memset(one[:], 1.0)
+        nc.scalar.activation(out=one[:], in_=one[:], func=FUNC.Sqrt)
+
+        def regroup_weight(grouped, raw):
+            nc.vector.tensor_copy(
+                out=grouped.rearrange("q (c t) -> q c t", t=PACK),
+                in_=raw.rearrange("q (t c) -> q c t", t=PACK),
+            )
+
+        def quantise(grouped, codes, scales):
+            nc.vector.quantize_mx(out=codes[:].bitcast(FP8X4), scales=scales[:], in_=grouped[:])
+
+        wc_grouped = consts.tile([P, D_LATENT * PACK], BF16, align_bytes=64)
+        wc_codes = consts.tile([P, D_LATENT], U32, align_bytes=64)
+        wc_scales = consts.tile([P, D_LATENT], U8, align_bytes=64)
+        regroup_weight(wc_grouped[:], wc_raw[:])
+        quantise(wc_grouped, wc_codes, wc_scales)
+
+        wkv_grouped = consts.tile([P, D_KV * PACK], BF16, align_bytes=64)
+        wkv_codes = consts.tile([P, D_KV], U32, align_bytes=64)
+        wkv_scales = consts.tile([P, D_KV], U8, align_bytes=64)
+        neg_sin = consts.tile([P, TILES_PER_BATCH * FREQS], BF16)
+
+        def prepare_up_weights():
+            nc.vector.tensor_copy(
+                out=wkv_grouped[:, 0 : D_K * PACK].rearrange("q (e m t) -> q e m t", e=2, t=PACK),
+                in_=wk_raw[:].rearrange("q (t m e) -> q e m t", t=PACK, e=2),
+            )
+            regroup_weight(wkv_grouped[:, D_K * PACK : D_KV * PACK], wv_raw[:])
+            nc.vector.tensor_scalar_mul(out=neg_sin[:], in0=sin_sb[:], scalar1=-1.0)
+            quantise(wkv_grouped, wkv_codes, wkv_scales)
+
+        x_mx, c_banks, rms_of, rstd_of, latent_of = {}, {}, {}, {}, {}
+        x_bank_of, latent_bank_of, x_grouped_of, latent_grouped_of = {}, {}, {}, {}
+        latent_mx, kv_bank_of, k_cos_of, k_sin_of = {}, {}, {}, {}
+
+        def transpose_words(bank, words):
+            for block in range(BANK_F32 // P):
+                cols = slice(block * P, (block + 1) * P)
+                nc.tensor.transpose(bank[:, cols], words[:, cols], ident[:])
+
+        def regroup_words(grouped, bank):
+            nc.scalar.copy(
+                out=grouped[:].bitcast(F32).rearrange("q (j n u) -> q j n u", j=ROUND_TILES, u=2),
+                in_=bank[:].rearrange("q (j u n) -> q j n u", j=ROUND_TILES, u=2),
+            )
+
+        def transpose_x(i):
+            x_bank = psum.tile([P, BANK_F32], F32)
+            words = x_chunks[i // CHUNK_ROUNDS][:].bitcast(F32)
+            first = (i % CHUNK_ROUNDS) * BANK_F32
+            transpose_words(x_bank, words[:, first : first + BANK_F32])
+            x_bank_of[i] = x_bank
+
+        def regroup_x(i):
+            x_grouped = work.tile([P, ROUND_TILES * P * PACK], BF16, align_bytes=64)
+            regroup_words(x_grouped, x_bank_of[i])
+            x_grouped_of[i] = x_grouped
+
+        def quantise_x(i):
+            x_codes = work.tile([P, ROUND_TILES * P], U32, align_bytes=64)
+            x_scales = work.tile([P, ROUND_TILES * P], U8, align_bytes=64)
+            quantise(x_grouped_of[i], x_codes, x_scales)
+            x_mx[i] = (x_codes, x_scales)
+
+        def compress(i):
+            codes, scales = x_mx[i]
+            c_banks[i] = []
+            for j in range(ROUND_TILES):
+                tokens = slice(j * P, (j + 1) * P)
+                c_bank = psum.tile([P, D_LATENT], F32, bufs=2 * ROUND_TILES)
+                nc.tensor.matmul_mx(
+                    out=c_bank[:],
+                    lhsT=codes[:, tokens].bitcast(FP8X4),
+                    lhsT_scale=scales[:, tokens],
+                    rhs=wc_codes[:].bitcast(FP8X4),
+                    rhs_scale=wc_scales[:],
+                    start=True,
+                    stop=True,
+                )
+                c_banks[i].append(c_bank)
+
+        def sum_squares(i):
+            sum_sq = work.tile([P, ROUND_TILES], F32)
+            for j in range(ROUND_TILES):
+                squares = work.tile([P, D_LATENT], BF16)
+                nc.scalar.activation(
+                    out=squares[:],
+                    in_=c_banks[i][j][:],
+                    func=FUNC.Square,
+                    accum_out=sum_sq[:, j : j + 1],
+                )
+            return sum_sq
+
+        def root_mean_square(i, sum_sq):
+            rms = work.tile([P, ROUND_TILES], F32)
+            nc.scalar.activation(
+                out=rms[:], in_=sum_sq[:], func=FUNC.Sqrt, scale=1.0 / D_LATENT, bias=EPS
+            )
+            rms_of[i] = rms
+
+        def reciprocal_rms(i):
+            rstd = work.tile([P, ROUND_TILES], F32)
+            nc.vector.reciprocal(out=rstd[:], in_=rms_of[i][:])
+            rstd_of[i] = rstd
+
+        def normalise(i):
+            latent = work.tile([P, ROUND_TILES * D_LATENT], BF16)
+            for j in range(ROUND_TILES):
+                nc.vector.scalar_tensor_tensor(
+                    out=latent[:, j * D_LATENT : (j + 1) * D_LATENT],
+                    in0=c_banks[i][j][:],
+                    scalar=rstd_of[i][:, j : j + 1],
+                    in1=gain[:],
+                    op0=ALU.mult,
+                    op1=ALU.mult,
+                )
+            latent_of[i] = latent
+
+        def transpose_latent(i):
+            latent_bank = psum.tile([P, BANK_F32], F32)
+            transpose_words(latent_bank, latent_of[i][:].bitcast(F32))
+            latent_bank_of[i] = latent_bank
+
+        def regroup_latent(i):
+            latent_grouped = work.tile([P, ROUND_TILES * P * PACK], BF16, align_bytes=64)
+            regroup_words(latent_grouped, latent_bank_of[i])
+            latent_grouped_of[i] = latent_grouped
+
+        def quantise_latent(i):
+            latent_codes = work.tile([P, ROUND_TILES * P], U32, align_bytes=64)
+            latent_scales = work.tile([P, ROUND_TILES * P], U8, align_bytes=64)
+            quantise(latent_grouped_of[i], latent_codes, latent_scales)
+            latent_mx[i] = (latent_codes, latent_scales)
+
+        def up_project(i):
+            codes, scales = latent_mx[i]
+            kv_bank = psum.tile([P, ROUND_TILES * D_KV], F32, bufs=2)
+            for j in range(ROUND_TILES):
+                tokens = slice(j * P, (j + 1) * P)
+                nc.tensor.matmul_mx(
+                    out=kv_bank[:, j * D_KV : (j + 1) * D_KV],
+                    lhsT=codes[:, tokens].bitcast(FP8X4),
+                    lhsT_scale=scales[:, tokens],
+                    rhs=wkv_codes[:].bitcast(FP8X4),
+                    rhs_scale=wkv_scales[:],
+                    start=True,
+                    stop=True,
+                )
+            kv_bank_of[i] = kv_bank
+
+        def table_of_round(table, i):
+            first = (i % ROUNDS_PER_BATCH) * ROUND_TILES * FREQS
+            rows = table[:, first : first + ROUND_TILES * FREQS]
+            return rows.rearrange("p (j f) -> p j f", j=ROUND_TILES).unsqueeze(2)
+
+        def rope_products(i):
+            kv = kv_bank_of[i][:].rearrange("p (j c) -> p j c", j=ROUND_TILES)
+            k_cos = work.tile([P, ROUND_TILES * D_K], F32)
+            k_sin = work.tile([P, ROUND_TILES * D_K], F32)
+            nc.vector.tensor_tensor(
+                out=k_cos[:].rearrange("p (j r f) -> p j r f", j=ROUND_TILES, f=FREQS),
+                in0=kv[:, :, 0:D_K].rearrange("p j (r f) -> p j r f", f=FREQS),
+                in1=table_of_round(cos_sb, i).to_broadcast([P, ROUND_TILES, 2 * HEADS, FREQS]),
+                op=ALU.mult,
+            )
+            k_sin_planes = k_sin[:].rearrange(
+                "p (j e h f) -> p j e h f", j=ROUND_TILES, e=2, h=HEADS
+            )
+            nc.vector.tensor_tensor(
+                out=k_sin_planes[:, :, 0],
+                in0=kv[:, :, PAIRS:D_K].rearrange("p j (h f) -> p j h f", h=HEADS),
+                in1=table_of_round(neg_sin, i).to_broadcast([P, ROUND_TILES, HEADS, FREQS]),
+                op=ALU.mult,
+            )
+            nc.vector.tensor_tensor(
+                out=k_sin_planes[:, :, 1],
+                in0=kv[:, :, 0:PAIRS].rearrange("p j (h f) -> p j h f", h=HEADS),
+                in1=table_of_round(sin_sb, i).to_broadcast([P, ROUND_TILES, HEADS, FREQS]),
+                op=ALU.mult,
+            )
+            k_cos_of[i] = k_cos
+            k_sin_of[i] = k_sin
+
+        def out_columns(i):
+            first = (i % ROUNDS_PER_BATCH) * ROUND_TILES * D_K
+            return slice(first, first + ROUND_TILES * D_K)
+
+        def copy_v(i):
+            kv = kv_bank_of[i][:].rearrange("p (j c) -> p j c", j=ROUND_TILES)
+            v_sb = work.tile([P, ROUND_TILES * D_K], F32)
+            nc.scalar.copy(
+                out=v_sb[:].rearrange("p (j c) -> p j c", j=ROUND_TILES), in_=kv[:, :, D_K:D_KV]
+            )
+            nc.sync.dma_start(out=v_rows[i // ROUNDS_PER_BATCH, :, out_columns(i)], in_=v_sb[:])
+
+        def rope_sum(i):
+            k_rot = work.tile([P, ROUND_TILES * D_K], F32)
+            nc.vector.tensor_tensor(
+                out=k_rot[:].rearrange("p (j m e) -> p j m e", j=ROUND_TILES, e=2),
+                in0=k_cos_of[i][:].rearrange("p (j e m) -> p j m e", j=ROUND_TILES, e=2),
+                in1=k_sin_of[i][:].rearrange("p (j e m) -> p j m e", j=ROUND_TILES, e=2),
+                op=ALU.add,
+            )
+            nc.sync.dma_start(out=k_rows[i // ROUNDS_PER_BATCH, :, out_columns(i)], in_=k_rot[:])
+
+        def in_range(i):
+            return 0 <= i < ROUNDS
+
+        def step(s):
+            if in_range(s - 1):
+                transpose_latent(s - 1)
+            if in_range(s + 2):
+                transpose_x(s + 2)
+            if in_range(s + 1):
+                compress(s + 1)
+            if in_range(s - 3):
+                up_project(s - 3)
+            if in_range(s - 4):
+                rope_products(s - 4)
+            if in_range(s):
+                sum_sq = sum_squares(s)
+            if in_range(s - 4):
+                copy_v(s - 4)
+            if in_range(s):
+                root_mean_square(s, sum_sq)
+            if in_range(s + 2):
+                regroup_x(s + 2)
+            if in_range(s - 1):
+                regroup_latent(s - 1)
+            if in_range(s - 2):
+                quantise_latent(s - 2)
+            if in_range(s):
+                reciprocal_rms(s)
+            if in_range(s - 4):
+                rope_sum(s - 4)
+            if in_range(s):
+                normalise(s)
+            if in_range(s + 2):
+                quantise_x(s + 2)
+
+        LOOK_AHEAD = 2
+        LAG = 4
+        for s in range(-LOOK_AHEAD, 0):
+            step(s)
+        prepare_up_weights()
+        for s in range(0, ROUNDS + LAG):
+            step(s)

@@ -39,7 +39,6 @@ def tile_mla_pa_t_kernel(
 ):
     nc = tc.nc
     with ExitStack() as stack:
-        stack.enter_context(tc.manual_schedule())
         consts = stack.enter_context(tc.tile_pool(name="consts", bufs=1))
         x_pool = stack.enter_context(tc.tile_pool(name="x_pool", bufs=CHUNKS))
         work = stack.enter_context(tc.tile_pool(name="work", bufs=3))
@@ -299,10 +298,10 @@ def tile_mla_pa_t_kernel(
             return 0 <= i < ROUNDS
 
         def step(s):
-            if in_range(s - 1):
-                transpose_latent(s - 1)
             if in_range(s + 2):
                 transpose_x(s + 2)
+            if in_range(s - 1):
+                transpose_latent(s - 1)
             if in_range(s + 1):
                 compress(s + 1)
             if in_range(s - 3):
@@ -310,23 +309,20 @@ def tile_mla_pa_t_kernel(
             if in_range(s - 4):
                 rope_products(s - 4)
             if in_range(s):
-                sum_sq = sum_squares(s)
-            if in_range(s - 4):
-                copy_v(s - 4)
-            if in_range(s):
-                root_mean_square(s, sum_sq)
+                root_mean_square(s, sum_squares(s))
             if in_range(s + 2):
                 regroup_x(s + 2)
             if in_range(s - 1):
                 regroup_latent(s - 1)
+            if in_range(s - 4):
+                copy_v(s - 4)
             if in_range(s - 2):
                 quantise_latent(s - 2)
             if in_range(s):
                 reciprocal_rms(s)
+                normalise(s)
             if in_range(s - 4):
                 rope_sum(s - 4)
-            if in_range(s):
-                normalise(s)
             if in_range(s + 2):
                 quantise_x(s + 2)
 

@@ -25,7 +25,7 @@ TILES_PER_BATCH = SEQ // P
 ROUND_TILES = 2
 ROUNDS_PER_BATCH = TILES_PER_BATCH // ROUND_TILES
 ROUNDS = BATCH * ROUNDS_PER_BATCH
-CHUNK_ROUNDS = 2
+CHUNK_ROUNDS = 1
 CHUNKS = ROUNDS // CHUNK_ROUNDS
 CHUNKS_PER_BATCH = CHUNKS // BATCH
 ROUND_X = ROUND_TILES * D_MODEL
@@ -70,26 +70,27 @@ def tile_mla_pa_t_kernel(
             )
             return x_chunk
 
-        load_weight(nc.sync, wc_raw, w_kv_compress)
         x_chunks = [load_x_chunk(0)]
+        load_weight(nc.sync, wc_raw, w_kv_compress)
+        x_chunks.append(load_x_chunk(1))
         load_weight(nc.sync, wk_raw, w_k_up)
         load_weight(nc.sync, wv_raw, w_v_up)
         nc.sync.dma_start(out=gain[:], in_=kv_norm_w.partition_broadcast(P))
-        x_chunks.append(load_x_chunk(1))
+        x_chunks.append(load_x_chunk(2))
         nc.sync.dma_start(
             out=cos_sb[:], in_=freqs_cos.rearrange("(p g) i -> p (g i)", g=TILES_PER_BATCH)
         )
         nc.sync.dma_start(
             out=sin_sb[:], in_=freqs_sin.rearrange("(p g) i -> p (g i)", g=TILES_PER_BATCH)
         )
-        for chunk in range(2, CHUNKS):
+        for chunk in range(3, CHUNKS):
             x_chunks.append(load_x_chunk(chunk))
 
         ident = consts.tile([P, P], F32)
         make_identity(nc, ident[:])
         one = consts.tile([P, 1], F32)
         nc.vector.memset(one[:], 1.0)
-        nc.scalar.activation(out=one[:], in_=one[:], func=FUNC.Sqrt)
+        nc.scalar.activation(out=one[:], in_=one[:], func=FUNC.Abs_reciprocal_sqrt)
 
         def regroup_weight(grouped, raw):
             nc.vector.tensor_copy(
@@ -120,7 +121,7 @@ def tile_mla_pa_t_kernel(
             nc.vector.tensor_scalar_mul(out=neg_sin[:], in0=sin_sb[:], scalar1=-1.0)
             quantise(wkv_grouped, wkv_codes, wkv_scales)
 
-        x_mx, c_banks, rms_of, rstd_of, latent_of = {}, {}, {}, {}, {}
+        x_mx, c_banks, rstd_of, latent_of = {}, {}, {}, {}
         x_bank_of, latent_bank_of, x_grouped_of, latent_grouped_of = {}, {}, {}, {}
         latent_mx, kv_bank_of, k_cos_of, k_sin_of = {}, {}, {}, {}
 
@@ -182,16 +183,15 @@ def tile_mla_pa_t_kernel(
                 )
             return sum_sq
 
-        def root_mean_square(i, sum_sq):
-            rms = work.tile([P, ROUND_TILES], F32)
-            nc.scalar.activation(
-                out=rms[:], in_=sum_sq[:], func=FUNC.Sqrt, scale=1.0 / D_LATENT, bias=EPS
-            )
-            rms_of[i] = rms
-
-        def reciprocal_rms(i):
+        def reciprocal_rms(i, sum_sq):
             rstd = work.tile([P, ROUND_TILES], F32)
-            nc.vector.reciprocal(out=rstd[:], in_=rms_of[i][:])
+            nc.scalar.activation(
+                out=rstd[:],
+                in_=sum_sq[:],
+                func=FUNC.Abs_reciprocal_sqrt,
+                scale=1.0 / D_LATENT,
+                bias=EPS,
+            )
             rstd_of[i] = rstd
 
         def normalise(i):
@@ -279,14 +279,13 @@ def tile_mla_pa_t_kernel(
         def copy_v(i):
             kv = kv_bank_of[i][:].rearrange("p (j c) -> p j c", j=ROUND_TILES)
             v_sb = work.tile([P, ROUND_TILES * D_K], F32)
-            nc.scalar.copy(
-                out=v_sb[:].rearrange("p (j c) -> p j c", j=ROUND_TILES), in_=kv[:, :, D_K:D_KV]
-            )
+            copy = nc.scalar.copy if i % 2 == 0 else nc.vector.tensor_copy
+            copy(out=v_sb[:].rearrange("p (j c) -> p j c", j=ROUND_TILES), in_=kv[:, :, D_K:D_KV])
             nc.sync.dma_start(out=v_rows[i // ROUNDS_PER_BATCH, :, out_columns(i)], in_=v_sb[:])
 
         def rope_sum(i):
             k_rot = work.tile([P, ROUND_TILES * D_K], F32)
-            nc.vector.tensor_tensor(
+            nc.gpsimd.tensor_tensor(
                 out=k_rot[:].rearrange("p (j m e) -> p j m e", j=ROUND_TILES, e=2),
                 in0=k_cos_of[i][:].rearrange("p (j e m) -> p j m e", j=ROUND_TILES, e=2),
                 in1=k_sin_of[i][:].rearrange("p (j e m) -> p j m e", j=ROUND_TILES, e=2),
@@ -309,7 +308,7 @@ def tile_mla_pa_t_kernel(
             if in_range(s - 4):
                 rope_products(s - 4)
             if in_range(s):
-                root_mean_square(s, sum_squares(s))
+                reciprocal_rms(s, sum_squares(s))
             if in_range(s + 2):
                 regroup_x(s + 2)
             if in_range(s - 1):
@@ -319,7 +318,6 @@ def tile_mla_pa_t_kernel(
             if in_range(s - 2):
                 quantise_latent(s - 2)
             if in_range(s):
-                reciprocal_rms(s)
                 normalise(s)
             if in_range(s - 4):
                 rope_sum(s - 4)

@@ -92,6 +92,23 @@ def tile_mla_pa_t_kernel(
         nc.vector.memset(one[:], 1.0)
         nc.scalar.activation(out=one[:], in_=one[:], func=FUNC.Abs_reciprocal_sqrt)
 
+        rotation = consts.tile([P, TILES_PER_BATCH * 2 * D_K], BF16)
+        rotation_parts = rotation[:].rearrange(
+            "p (g o e h f) -> p g o e h f", g=TILES_PER_BATCH, o=2, e=2, h=HEADS
+        )
+        for o, e, table, sign in ((0, 0, cos_sb, 1.0), (0, 1, sin_sb, -1.0), (1, 0, sin_sb, 1.0), (1, 1, cos_sb, 1.0)):
+            nc.gpsimd.tensor_scalar(
+                out=rotation_parts[:, :, o, e],
+                in0=table[:]
+                .rearrange("p (g f) -> p g f", g=TILES_PER_BATCH)
+                .unsqueeze(2)
+                .to_broadcast([P, TILES_PER_BATCH, HEADS, FREQS]),
+                scalar1=sign,
+                scalar2=0.0,
+                op0=ALU.mult,
+                op1=ALU.add,
+            )
+
         def regroup_weight(grouped, raw):
             nc.vector.tensor_copy(
                 out=grouped.rearrange("q (c t) -> q c t", t=PACK),
@@ -110,7 +127,6 @@ def tile_mla_pa_t_kernel(
         wkv_grouped = consts.tile([P, D_KV * PACK], BF16, align_bytes=64)
         wkv_codes = consts.tile([P, D_KV], U32, align_bytes=64)
         wkv_scales = consts.tile([P, D_KV], U8, align_bytes=64)
-        neg_sin = consts.tile([P, TILES_PER_BATCH * FREQS], BF16)
 
         def prepare_up_weights():
             nc.vector.tensor_copy(
@@ -118,12 +134,11 @@ def tile_mla_pa_t_kernel(
                 in_=wk_raw[:].rearrange("q (t m e) -> q e m t", t=PACK, e=2),
             )
             regroup_weight(wkv_grouped[:, D_K * PACK : D_KV * PACK], wv_raw[:])
-            nc.vector.tensor_scalar_mul(out=neg_sin[:], in0=sin_sb[:], scalar1=-1.0)
             quantise(wkv_grouped, wkv_codes, wkv_scales)
 
         x_mx, c_banks, rstd_of, latent_of = {}, {}, {}, {}
         x_bank_of, latent_bank_of, x_grouped_of, latent_grouped_of = {}, {}, {}, {}
-        latent_mx, kv_bank_of, k_cos_of, k_sin_of = {}, {}, {}, {}
+        latent_mx, kv_bank_of, products_of = {}, {}, {}
 
         def transpose_words(bank, words):
             for block in range(BANK_F32 // P):
@@ -239,38 +254,19 @@ def tile_mla_pa_t_kernel(
                 )
             kv_bank_of[i] = kv_bank
 
-        def table_of_round(table, i):
-            first = (i % ROUNDS_PER_BATCH) * ROUND_TILES * FREQS
-            rows = table[:, first : first + ROUND_TILES * FREQS]
-            return rows.rearrange("p (j f) -> p j f", j=ROUND_TILES).unsqueeze(2)
-
         def rope_products(i):
             kv = kv_bank_of[i][:].rearrange("p (j c) -> p j c", j=ROUND_TILES)
-            k_cos = work.tile([P, ROUND_TILES * D_K], F32)
-            k_sin = work.tile([P, ROUND_TILES * D_K], F32)
+            first = (i % ROUNDS_PER_BATCH) * ROUND_TILES * 2 * D_K
+            products = work.tile([P, ROUND_TILES * 2 * D_K], F32)
             nc.vector.tensor_tensor(
-                out=k_cos[:].rearrange("p (j r f) -> p j r f", j=ROUND_TILES, f=FREQS),
-                in0=kv[:, :, 0:D_K].rearrange("p j (r f) -> p j r f", f=FREQS),
-                in1=table_of_round(cos_sb, i).to_broadcast([P, ROUND_TILES, 2 * HEADS, FREQS]),
+                out=products[:].rearrange("p (j o c) -> p j o c", j=ROUND_TILES, o=2),
+                in0=kv[:, :, 0:D_K].unsqueeze(2).to_broadcast([P, ROUND_TILES, 2, D_K]),
+                in1=rotation[:, first : first + ROUND_TILES * 2 * D_K].rearrange(
+                    "p (j o c) -> p j o c", j=ROUND_TILES, o=2
+                ),
                 op=ALU.mult,
             )
-            k_sin_planes = k_sin[:].rearrange(
-                "p (j e h f) -> p j e h f", j=ROUND_TILES, e=2, h=HEADS
-            )
-            nc.vector.tensor_tensor(
-                out=k_sin_planes[:, :, 0],
-                in0=kv[:, :, PAIRS:D_K].rearrange("p j (h f) -> p j h f", h=HEADS),
-                in1=table_of_round(neg_sin, i).to_broadcast([P, ROUND_TILES, HEADS, FREQS]),
-                op=ALU.mult,
-            )
-            nc.vector.tensor_tensor(
-                out=k_sin_planes[:, :, 1],
-                in0=kv[:, :, 0:PAIRS].rearrange("p j (h f) -> p j h f", h=HEADS),
-                in1=table_of_round(sin_sb, i).to_broadcast([P, ROUND_TILES, HEADS, FREQS]),
-                op=ALU.mult,
-            )
-            k_cos_of[i] = k_cos
-            k_sin_of[i] = k_sin
+            products_of[i] = products
 
         def out_columns(i):
             first = (i % ROUNDS_PER_BATCH) * ROUND_TILES * D_K
@@ -284,11 +280,14 @@ def tile_mla_pa_t_kernel(
             nc.sync.dma_start(out=v_rows[i // ROUNDS_PER_BATCH, :, out_columns(i)], in_=v_sb[:])
 
         def rope_sum(i):
+            planes = products_of[i][:].rearrange(
+                "p (j o e m) -> p e j m o", j=ROUND_TILES, o=2, e=2
+            )
             k_rot = work.tile([P, ROUND_TILES * D_K], F32)
             nc.gpsimd.tensor_tensor(
-                out=k_rot[:].rearrange("p (j m e) -> p j m e", j=ROUND_TILES, e=2),
-                in0=k_cos_of[i][:].rearrange("p (j e m) -> p j m e", j=ROUND_TILES, e=2),
-                in1=k_sin_of[i][:].rearrange("p (j e m) -> p j m e", j=ROUND_TILES, e=2),
+                out=k_rot[:].rearrange("p (j m o) -> p j m o", j=ROUND_TILES, o=2),
+                in0=planes[:, 0],
+                in1=planes[:, 1],
                 op=ALU.add,
             )
             nc.sync.dma_start(out=k_rows[i // ROUNDS_PER_BATCH, :, out_columns(i)], in_=k_rot[:])

@@ -275,8 +275,9 @@ def tile_mla_pa_t_kernel(
         def copy_v(i):
             kv = kv_bank_of[i][:].rearrange("p (j c) -> p j c", j=ROUND_TILES)
             v_sb = work.tile([P, ROUND_TILES * D_K], F32)
-            copy = nc.scalar.copy if i % 2 == 0 else nc.vector.tensor_copy
-            copy(out=v_sb[:].rearrange("p (j c) -> p j c", j=ROUND_TILES), in_=kv[:, :, D_K:D_KV])
+            nc.vector.tensor_copy(
+                out=v_sb[:].rearrange("p (j c) -> p j c", j=ROUND_TILES), in_=kv[:, :, D_K:D_KV]
+            )
             nc.sync.dma_start(out=v_rows[i // ROUNDS_PER_BATCH, :, out_columns(i)], in_=v_sb[:])
 
         def rope_sum(i):
@@ -306,14 +307,13 @@ def tile_mla_pa_t_kernel(
                 up_project(s - 3)
             if in_range(s - 4):
                 rope_products(s - 4)
+                copy_v(s - 4)
             if in_range(s):
                 reciprocal_rms(s, sum_squares(s))
             if in_range(s + 2):
                 regroup_x(s + 2)
             if in_range(s - 1):
                 regroup_latent(s - 1)
-            if in_range(s - 4):
-                copy_v(s - 4)
             if in_range(s - 2):
                 quantise_latent(s - 2)
             if in_range(s):

from contextlib import ExitStack

import concourse.mybir as mybir
from concourse.masks import make_identity

F32 = mybir.dt.float32
BF16 = mybir.dt.bfloat16
U32 = mybir.dt.uint32
U8 = mybir.dt.uint8
FP8X4 = mybir.dt.float8_e4m3fn_x4
FUNC = mybir.ActivationFunctionType
ALU = mybir.AluOpType

P = 128
PACK = 4
BATCH, SEQ, D_MODEL, D_LATENT = 4, 2048, 512, 512
HEADS, D_HEAD = 2, 64
D_K = HEADS * D_HEAD
D_KV = 2 * D_K
FREQS = D_HEAD // 2
PAIRS = HEADS * FREQS
EPS = 1e-6

TILES_PER_BATCH = SEQ // P
ROUND_TILES = 2
ROUNDS_PER_BATCH = TILES_PER_BATCH // ROUND_TILES
ROUNDS = BATCH * ROUNDS_PER_BATCH
CHUNK_ROUNDS = 1
CHUNKS = ROUNDS // CHUNK_ROUNDS
CHUNKS_PER_BATCH = CHUNKS // BATCH
ROUND_X = ROUND_TILES * D_MODEL
BANK_F32 = 512

FLOPS = 2 * BATCH * SEQ * D_MODEL * D_LATENT + 2 * BATCH * SEQ * D_LATENT * D_KV


def tile_mla_pa_t_kernel(
    tc, x, freqs_cos, freqs_sin, w_kv_compress, kv_norm_w, w_k_up, w_v_up, out_0, out_1
):
    nc = tc.nc
    with ExitStack() as stack:
        consts = stack.enter_context(tc.tile_pool(name="consts", bufs=1))
        x_pool = stack.enter_context(tc.tile_pool(name="x_pool", bufs=CHUNKS))
        work = stack.enter_context(tc.tile_pool(name="work", bufs=3))
        psum = stack.enter_context(tc.psum_pool(name="psum", bufs=1))

        x_rows = x.rearrange("b (p g) d -> b p (g d)", g=TILES_PER_BATCH)
        k_rows = out_0.rearrange("b (p g) h d -> b p (g h d)", g=TILES_PER_BATCH)
        v_rows = out_1.rearrange("b (p g) h d -> b p (g h d)", g=TILES_PER_BATCH)

        def load_weight(queue, raw, weight):
            queue.dma_start(
                out=raw[:].rearrange("q (u ec) -> q u ec", u=2),
                in_=weight.rearrange("(u q e) c -> q u (e c)", u=2, e=2),
            )

        wc_raw = consts.tile([P, PACK * D_LATENT], BF16)
        wk_raw = consts.tile([P, PACK * D_K], BF16)
        wv_raw = consts.tile([P, PACK * D_K], BF16)
        gain = consts.tile([P, D_LATENT], BF16)
        cos_sb = consts.tile([P, TILES_PER_BATCH * FREQS], BF16)
        sin_sb = consts.tile([P, TILES_PER_BATCH * FREQS], BF16)

        def load_x_chunk(chunk):
            x_chunk = x_pool.tile([P, CHUNK_ROUNDS * ROUND_X], BF16)
            first = (chunk % CHUNKS_PER_BATCH) * CHUNK_ROUNDS * ROUND_X
            nc.sync.dma_start(
                out=x_chunk[:],
                in_=x_rows[chunk // CHUNKS_PER_BATCH, :, first : first + CHUNK_ROUNDS * ROUND_X],
            )
            return x_chunk

        x_chunks = [load_x_chunk(0)]
        load_weight(nc.sync, wc_raw, w_kv_compress)
        x_chunks.append(load_x_chunk(1))
        load_weight(nc.sync, wk_raw, w_k_up)
        load_weight(nc.sync, wv_raw, w_v_up)
        nc.sync.dma_start(out=gain[:], in_=kv_norm_w.partition_broadcast(P))
        x_chunks.append(load_x_chunk(2))
        nc.sync.dma_start(
            out=cos_sb[:], in_=freqs_cos.rearrange("(p g) i -> p (g i)", g=TILES_PER_BATCH)
        )
        nc.sync.dma_start(
            out=sin_sb[:], in_=freqs_sin.rearrange("(p g) i -> p (g i)", g=TILES_PER_BATCH)
        )
        for chunk in range(3, CHUNKS):
            x_chunks.append(load_x_chunk(chunk))

        ident = consts.tile([P, P], F32)
        make_identity(nc, ident[:])
        one = consts.tile([P, 1], F32)
        nc.vector.memset(one[:], 1.0)
        nc.scalar.activation(out=one[:], in_=one[:], func=FUNC.Abs_reciprocal_sqrt)

        rotation = consts.tile([P, TILES_PER_BATCH * 2 * D_K], BF16)
        rotation_parts = rotation[:].rearrange(
            "p (g o e h f) -> p g o e h f", g=TILES_PER_BATCH, o=2, e=2, h=HEADS
        )
        for o, e, table, sign in ((0, 0, cos_sb, 1.0), (0, 1, sin_sb, -1.0), (1, 0, sin_sb, 1.0), (1, 1, cos_sb, 1.0)):
            nc.gpsimd.tensor_scalar(
                out=rotation_parts[:, :, o, e],
                in0=table[:]
                .rearrange("p (g f) -> p g f", g=TILES_PER_BATCH)
                .unsqueeze(2)
                .to_broadcast([P, TILES_PER_BATCH, HEADS, FREQS]),
                scalar1=sign,
                scalar2=0.0,
                op0=ALU.mult,
                op1=ALU.add,
            )

        def regroup_weight(grouped, raw):
            nc.vector.tensor_copy(
                out=grouped.rearrange("q (c t) -> q c t", t=PACK),
                in_=raw.rearrange("q (t c) -> q c t", t=PACK),
            )

        def quantise(grouped, codes, scales):
            nc.vector.quantize_mx(out=codes[:].bitcast(FP8X4), scales=scales[:], in_=grouped[:])

        wc_grouped = consts.tile([P, D_LATENT * PACK], BF16, align_bytes=64)
        wc_codes = consts.tile([P, D_LATENT], U32, align_bytes=64)
        wc_scales = consts.tile([P, D_LATENT], U8, align_bytes=64)
        regroup_weight(wc_grouped[:], wc_raw[:])
        quantise(wc_grouped, wc_codes, wc_scales)

        wkv_grouped = consts.tile([P, D_KV * PACK], BF16, align_bytes=64)
        wkv_codes = consts.tile([P, D_KV], U32, align_bytes=64)
        wkv_scales = consts.tile([P, D_KV], U8, align_bytes=64)

        def prepare_up_weights():
            nc.vector.tensor_copy(
                out=wkv_grouped[:, 0 : D_K * PACK].rearrange("q (e m t) -> q e m t", e=2, t=PACK),
                in_=wk_raw[:].rearrange("q (t m e) -> q e m t", t=PACK, e=2),
            )
            regroup_weight(wkv_grouped[:, D_K * PACK : D_KV * PACK], wv_raw[:])
            quantise(wkv_grouped, wkv_codes, wkv_scales)

        x_mx, c_banks, rstd_of, latent_of = {}, {}, {}, {}
        x_bank_of, latent_bank_of, x_grouped_of, latent_grouped_of = {}, {}, {}, {}
        latent_mx, kv_bank_of, products_of = {}, {}, {}

        def transpose_words(bank, words):
            for block in range(BANK_F32 // P):
                cols = slice(block * P, (block + 1) * P)
                nc.tensor.transpose(bank[:, cols], words[:, cols], ident[:])

        def regroup_words(grouped, bank):
            nc.scalar.copy(
                out=grouped[:].bitcast(F32).rearrange("q (j n u) -> q j n u", j=ROUND_TILES, u=2),
                in_=bank[:].rearrange("q (j u n) -> q j n u", j=ROUND_TILES, u=2),
            )

        def transpose_x(i):
            x_bank = psum.tile([P, BANK_F32], F32)
            words = x_chunks[i // CHUNK_ROUNDS][:].bitcast(F32)
            first = (i % CHUNK_ROUNDS) * BANK_F32
            transpose_words(x_bank, words[:, first : first + BANK_F32])
            x_bank_of[i] = x_bank

        def regroup_x(i):
            x_grouped = work.tile([P, ROUND_TILES * P * PACK], BF16, align_bytes=64)
            regroup_words(x_grouped, x_bank_of[i])
            x_grouped_of[i] = x_grouped

        def quantise_x(i):
            x_codes = work.tile([P, ROUND_TILES * P], U32, align_bytes=64)
            x_scales = work.tile([P, ROUND_TILES * P], U8, align_bytes=64)
            quantise(x_grouped_of[i], x_codes, x_scales)
            x_mx[i] = (x_codes, x_scales)

        def compress(i):
            codes, scales = x_mx[i]
            c_banks[i] = []
            for j in range(ROUND_TILES):
                tokens = slice(j * P, (j + 1) * P)
                c_bank = psum.tile([P, D_LATENT], F32, bufs=2 * ROUND_TILES)
                nc.tensor.matmul_mx(
                    out=c_bank[:],
                    lhsT=codes[:, tokens].bitcast(FP8X4),
                    lhsT_scale=scales[:, tokens],
                    rhs=wc_codes[:].bitcast(FP8X4),
                    rhs_scale=wc_scales[:],
                    start=True,
                    stop=True,
                )
                c_banks[i].append(c_bank)

        def sum_squares(i):
            sum_sq = work.tile([P, ROUND_TILES], F32)
            for j in range(ROUND_TILES):
                squares = work.tile([P, D_LATENT], BF16)
                nc.scalar.activation(
                    out=squares[:],
                    in_=c_banks[i][j][:],
                    func=FUNC.Square,
                    accum_out=sum_sq[:, j : j + 1],
                )
            return sum_sq

        def reciprocal_rms(i, sum_sq):
            rstd = work.tile([P, ROUND_TILES], F32)
            nc.scalar.activation(
                out=rstd[:],
                in_=sum_sq[:],
                func=FUNC.Abs_reciprocal_sqrt,
                scale=1.0 / D_LATENT,
                bias=EPS,
            )
            rstd_of[i] = rstd

        def normalise(i):
            latent = work.tile([P, ROUND_TILES * D_LATENT], BF16)
            for j in range(ROUND_TILES):
                nc.vector.scalar_tensor_tensor(
                    out=latent[:, j * D_LATENT : (j + 1) * D_LATENT],
                    in0=c_banks[i][j][:],
                    scalar=rstd_of[i][:, j : j + 1],
                    in1=gain[:],
                    op0=ALU.mult,
                    op1=ALU.mult,
                )
            latent_of[i] = latent

        def transpose_latent(i):
            latent_bank = psum.tile([P, BANK_F32], F32)
            transpose_words(latent_bank, latent_of[i][:].bitcast(F32))
            latent_bank_of[i] = latent_bank

        def regroup_latent(i):
            latent_grouped = work.tile([P, ROUND_TILES * P * PACK], BF16, align_bytes=64)
            regroup_words(latent_grouped, latent_bank_of[i])
            latent_grouped_of[i] = latent_grouped

        def quantise_latent(i):
            latent_codes = work.tile([P, ROUND_TILES * P], U32, align_bytes=64)
            latent_scales = work.tile([P, ROUND_TILES * P], U8, align_bytes=64)
            quantise(latent_grouped_of[i], latent_codes, latent_scales)
            latent_mx[i] = (latent_codes, latent_scales)

        def up_project(i):
            codes, scales = latent_mx[i]
            kv_bank = psum.tile([P, ROUND_TILES * D_KV], F32, bufs=2)
            for j in range(ROUND_TILES):
                tokens = slice(j * P, (j + 1) * P)
                nc.tensor.matmul_mx(
                    out=kv_bank[:, j * D_KV : (j + 1) * D_KV],
                    lhsT=codes[:, tokens].bitcast(FP8X4),
                    lhsT_scale=scales[:, tokens],
                    rhs=wkv_codes[:].bitcast(FP8X4),
                    rhs_scale=wkv_scales[:],
                    start=True,
                    stop=True,
                )
            kv_bank_of[i] = kv_bank

        def rope_products(i):
            kv = kv_bank_of[i][:].rearrange("p (j c) -> p j c", j=ROUND_TILES)
            first = (i % ROUNDS_PER_BATCH) * ROUND_TILES * 2 * D_K
            products = work.tile([P, ROUND_TILES * 2 * D_K], F32)
            nc.vector.tensor_tensor(
                out=products[:].rearrange("p (j o c) -> p j o c", j=ROUND_TILES, o=2),
                in0=kv[:, :, 0:D_K].unsqueeze(2).to_broadcast([P, ROUND_TILES, 2, D_K]),
                in1=rotation[:, first : first + ROUND_TILES * 2 * D_K].rearrange(
                    "p (j o c) -> p j o c", j=ROUND_TILES, o=2
                ),
                op=ALU.mult,
            )
            products_of[i] = products

        def out_columns(i):
            first = (i % ROUNDS_PER_BATCH) * ROUND_TILES * D_K
            return slice(first, first + ROUND_TILES * D_K)

        def copy_v(i):
            kv = kv_bank_of[i][:].rearrange("p (j c) -> p j c", j=ROUND_TILES)
            v_sb = work.tile([P, ROUND_TILES * D_K], F32)
            nc.vector.tensor_copy(
                out=v_sb[:].rearrange("p (j c) -> p j c", j=ROUND_TILES), in_=kv[:, :, D_K:D_KV]
            )
            nc.sync.dma_start(out=v_rows[i // ROUNDS_PER_BATCH, :, out_columns(i)], in_=v_sb[:])

        def rope_sum(i):
            planes = products_of[i][:].rearrange(
                "p (j o e m) -> p e j m o", j=ROUND_TILES, o=2, e=2
            )
            k_rot = work.tile([P, ROUND_TILES * D_K], F32)
            nc.gpsimd.tensor_tensor(
                out=k_rot[:].rearrange("p (j m o) -> p j m o", j=ROUND_TILES, o=2),
                in0=planes[:, 0],
                in1=planes[:, 1],
                op=ALU.add,
            )
            nc.sync.dma_start(out=k_rows[i // ROUNDS_PER_BATCH, :, out_columns(i)], in_=k_rot[:])

        def in_range(i):
            return 0 <= i < ROUNDS

        def step(s):
            if in_range(s + 2):
                transpose_x(s + 2)
            if in_range(s - 1):
                transpose_latent(s - 1)
            if in_range(s + 1):
                compress(s + 1)
            if in_range(s - 3):
                up_project(s - 3)
            if in_range(s - 4):
                rope_products(s - 4)
                copy_v(s - 4)
            if in_range(s):
                reciprocal_rms(s, sum_squares(s))
            if in_range(s + 2):
                regroup_x(s + 2)
            if in_range(s - 1):
                regroup_latent(s - 1)
            if in_range(s - 2):
                quantise_latent(s - 2)
            if in_range(s):
                normalise(s)
            if in_range(s - 4):
                rope_sum(s - 4)
            if in_range(s + 2):
                quantise_x(s + 2)

        LOOK_AHEAD = 2
        LAG = 4
        for s in range(-LOOK_AHEAD, 0):
            step(s)
        prepare_up_weights()
        for s in range(0, ROUNDS + LAG):
            step(s)
